import numpy as np
import ml_dtypes


def mxq(x, axis, fmt="e4m3"):
    dtype, down = {"e4m3": (ml_dtypes.float8_e4m3fn, 7), "e5m2": (ml_dtypes.float8_e5m2, 14)}[fmt]
    v = np.moveaxis(np.asarray(x, np.float32).astype(ml_dtypes.bfloat16).astype(np.float64), axis, -1)
    blocks = v.reshape(v.shape[:-1] + (-1, 32))
    amax = np.abs(blocks).max(-1, keepdims=True)
    byte = np.maximum(np.where(amax > 0, np.frexp(amax)[1] - 1 + 127, 0) - down, 1)
    scale = np.exp2(byte - 127.0)
    codes = (blocks / scale).astype(np.float32).astype(dtype).astype(np.float64)
    return np.moveaxis((codes * scale).reshape(v.shape), -1, axis)


WIDE = False


def mx_kscale(k):
    if not WIDE:
        return np.ones(k)
    levels = np.array([10, -10, 5, -5, 0])
    a = np.random.permutation(np.resize(levels, k // 512 * 4)).reshape(k // 512, 4)
    idx = np.arange(k)
    return np.exp2(a[idx // 512, idx % 128 // 32])


BF16 = ml_dtypes.bfloat16


def bf(x):
    return np.asarray(x, np.float32).astype(BF16)


def f64(x):
    return np.asarray(x).astype(np.float64)


E2M1 = np.array([0.0, 0.5, 1.0, 1.5, 2.0, 3.0, 4.0, 6.0, -0.0, -0.5, -1.0, -1.5, -2.0, -3.0, -4.0, -6.0])


def pack_weight(w, fmt):
    k, n = w.shape
    w = f64(bf(w)).reshape(k // 32, 32, n)
    amax = np.abs(w).max(1)
    if fmt == "e4m3":
        byte = np.frexp(amax)[1] - 1 + 127 - 7
    else:
        mant, ex = np.frexp(amax / 6.0)
        byte = np.where(mant > 0.5, ex, ex - 1) + 127
    byte = np.clip(np.where(amax > 0, byte, 1), 1, 254)
    scaled = (w * np.exp2(127.0 - byte)[:, None, :]).reshape(k, n).astype(np.float32)
    by_word = np.ascontiguousarray(scaled.reshape(k // 512, 128, 4, n).transpose(0, 1, 3, 2))
    if fmt == "e4m3":
        words = by_word.astype(ml_dtypes.float8_e4m3fn).view(np.uint8)
    else:
        c = by_word.astype(ml_dtypes.float4_e2m1fn).view(np.uint8) & 0xF
        words = c[..., 0::2] | (c[..., 1::2] << 4)
    return np.ascontiguousarray(words), np.ascontiguousarray(byte.astype(np.uint8).reshape(k // 512, 16, n))


def unpack_weight(words, scales, fmt):
    g, p, n, _ = words.shape
    if fmt == "e4m3":
        vals = np.ascontiguousarray(words).view(ml_dtypes.float8_e4m3fn).astype(np.float64)
    else:
        nib = np.empty((g, p, n, 4), np.uint8)
        nib[..., 0::2] = words & 0xF
        nib[..., 1::2] = words >> 4
        vals = E2M1[nib]
    vals = vals * np.repeat(np.exp2(scales.astype(np.float64) - 127.0), 8, axis=1)[..., None]
    return vals.transpose(0, 1, 3, 2).reshape(g * 512, n)

def pack4(w):
    words, scales = pack_weight(w, "e2m1")
    return words.reshape(words.shape[0], 128, -1), scales


def unpack4(words, scales):
    return unpack_weight(words.reshape(words.shape[0], 128, -1, 2), scales, "e2m1")


B, S, H = 4, 1025, 512
N = B * (S - 1)
G = 0.75


def setup_inputs():
    s = mx_kscale(H)
    x = bf(np.random.standard_normal((B, S, H)) * s)
    k1 = bf(np.random.standard_normal((N, H)) * G * s)
    k2 = bf(np.random.standard_normal((N, H)) * G * np.sqrt(1.0 + 0.25 * G * G) * s)
    coefficients = np.random.standard_normal((H, H)) * G / np.sqrt(H) * s[:, None] / s[None, :]
    words, scales = pack4(np.ascontiguousarray(coefficients.T))
    return {"x": x,
            "k1": k1,
            "k2": k2,
            "coefficients_words": words,
            "coefficients_scales": scales}


def reference(x, k1, k2, coefficients_words, coefficients_scales):
    x, k1, k2 = f64(x), f64(k1), f64(k2)
    y = x[:, :-1, :].reshape(-1, H)
    ct = unpack4(coefficients_words, coefficients_scales)
    k3 = mxq(y + 0.5 * k2, 1, "e4m3") @ ct
    k4 = mxq(y + k3, 1, "e4m3") @ ct
    y1 = y + (k1 + 2.0 * k2 + 2.0 * k3 + k4) / 6.0
    return y1.reshape(B, S - 1, H) - x[:, 1:, :]

@@ -1,0 +1,220 @@
+from contextlib import ExitStack
+
+import concourse.mybir as mybir
+from concourse.masks import make_identity
+
+F32 = mybir.dt.float32
+BF16 = mybir.dt.bfloat16
+I32 = mybir.dt.int32
+U32 = mybir.dt.uint32
+U8 = mybir.dt.uint8
+FP8X4 = mybir.dt.float8_e4m3fn_x4
+FP4X4 = mybir.dt.float4_e2m1fn_x4
+ADD = mybir.AluOpType.add
+SUB = mybir.AluOpType.subtract
+MULT = mybir.AluOpType.mult
+
+P = 128
+SEQS = 4
+STEPS = 1024
+H = 512
+PACK = 4
+ROWS_PP = STEPS // P
+CHUNK = 4
+HALVES = ROWS_PP // CHUNK
+N_CHUNKS = SEQS * HALVES
+PAIR = 2
+
+FLOPS = 2 * 2 * SEQS * STEPS * H * H
+
+
+def tile_sindylossmixin_pa_t_kernel(
+    tc, x, k1, k2, coefficients_words, coefficients_scales, out
+):
+    nc = tc.nc
+
+    def by_partition(rows):
+        return rows.rearrange("(p j) f -> p j f", j=ROWS_PP)
+
+    with ExitStack() as stack:
+        stack.enter_context(tc.manual_schedule())
+        keep = stack.enter_context(tc.tile_pool(name="keep", bufs=1))
+        work = stack.enter_context(tc.tile_pool(name="work", bufs=2))
+        sums = stack.enter_context(tc.tile_pool(name="sums", bufs=4))
+        bank_tr = stack.enter_context(tc.psum_pool(name="bank_tr", bufs=2))
+        bank_k3 = stack.enter_context(tc.psum_pool(name="bank_k3", bufs=2))
+        bank_kk = stack.enter_context(tc.psum_pool(name="bank_kk", bufs=4))
+
+        x_sb = keep.tile([P, SEQS, ROWS_PP + 1, H], BF16)
+        k1_sb = keep.tile([P, SEQS, ROWS_PP, H], BF16)
+        k2_sb = keep.tile([P, SEQS, ROWS_PP, H], BF16)
+        w_words = keep.tile([P, 2 * H], U8, align_bytes=64)
+        w_scales = keep.tile([P, H], U8, align_bytes=64)
+        ident = keep.tile([P, P], F32)
+
+        def place(c):
+            return c // HALVES, CHUNK * (c % HALVES)
+
+        def load(dst, src, c):
+            b, j0 = place(c)
+            nc.sync.dma_start(out=dst[:, b, j0 : j0 + CHUNK, :], in_=src[:, j0 : j0 + CHUNK, :])
+
+        def load_x(c):
+            b, j0 = place(c)
+            load(x_sb, by_partition(x[b, 0:STEPS, :]), c)
+            if j0 + CHUNK == ROWS_PP:
+                nc.sync.dma_start(
+                    out=x_sb[:, b, ROWS_PP, :],
+                    in_=by_partition(x[b, 1 : STEPS + 1, :])[:, ROWS_PP - 1, :],
+                )
+
+        def load_k(dst, src, c):
+            b, j0 = place(c)
+            load(dst, by_partition(src[b * STEPS : (b + 1) * STEPS, :]), c)
+
+        nc.vector.memset(w_scales[:].bitcast(I32), 0)
+        make_identity(nc, ident[:])
+        load_x(0)
+        load_k(k2_sb, k2, 0)
+        nc.sync.dma_start(out=w_words[:].bitcast(I32), in_=coefficients_words[0].bitcast(I32))
+        for quad in range(4):
+            nc.sync.dma_start(
+                out=w_scales[32 * quad : 32 * quad + 4, :].bitcast(I32),
+                in_=coefficients_scales[0, 4 * quad : 4 * quad + 4, :].bitcast(I32),
+            )
+        load_k(k1_sb, k1, 0)
+        for c in range(1, N_CHUNKS):
+            load_x(c)
+            load_k(k2_sb, k2, c)
+            load_k(k1_sb, k1, c)
+
+        half_k2 = {}
+        arg = {}
+        grouped = {}
+        codes = {}
+        scales = {}
+        total = {}
+
+        def y_of(c):
+            b, j0 = place(c)
+            return x_sb[:, b, j0 : j0 + CHUNK, :]
+
+        def halve_k2(c):
+            b, j0 = place(c)
+            h = work.tile([P, CHUNK, H], BF16, tag="half_k2")
+            nc.scalar.mul(h[:], k2_sb[:, b, j0 : j0 + CHUNK, :], 0.5)
+            half_k2[c] = h
+
+        def first_argument(c):
+            a = work.tile([P, CHUNK, H], BF16, tag="arg1")
+            nc.vector.tensor_tensor(out=a[:], in0=y_of(c), in1=half_k2[c][:], op=ADD)
+            arg[1, c] = a
+
+        def turn(stage, c):
+            g = work.tile([P, CHUNK, P, PACK], BF16, tag="grouped%d" % stage, align_bytes=64)
+            for i0 in range(0, CHUNK, PAIR):
+                tr = bank_tr.tile([P, PAIR, 2, P], F32)
+                for i in range(PAIR):
+                    words = arg[stage, c][:, i0 + i, :].bitcast(F32)
+                    for u in range(2):
+                        nc.tensor.transpose(tr[:, i, u, :], words[:, u : H // 2 : 2], ident[:])
+                nc.scalar.copy(
+                    out=g[:, i0 : i0 + PAIR, :, :].bitcast(F32),
+                    in_=tr[:].rearrange("p i u r -> p i r u"),
+                )
+            grouped[stage, c] = g
+
+        def quantise(stage, c):
+            q = work.tile([P, CHUNK * P], U32, tag="codes%d" % stage, bufs=3, align_bytes=64)
+            s = work.tile([P, CHUNK * P], U8, tag="scales%d" % stage, bufs=3, align_bytes=64)
+            nc.vector.quantize_mx(
+                out=q[:].bitcast(FP8X4),
+                scales=s[:],
+                in_=grouped[stage, c][:].rearrange("p i r t -> p (i r t)"),
+            )
+            codes[stage, c] = q
+            scales[stage, c] = s
+
+        def product(acc, stage, c, i, start, stop):
+            rows = slice(i * P, (i + 1) * P)
+            nc.tensor.matmul_mx(
+                out=acc[:],
+                lhsT=codes[stage, c][:, rows].bitcast(FP8X4),
+                lhsT_scale=scales[stage, c][:, rows],
+                rhs=w_words[:].bitcast(FP4X4),
+                rhs_scale=w_scales[:],
+                start=start,
+                stop=stop,
+            )
+
+        def second_argument(c):
+            a = work.tile([P, CHUNK, H], BF16, tag="arg2")
+            for i in range(CHUNK):
+                k3 = bank_k3.tile([P, H], F32)
+                product(k3, 1, c, i, True, True)
+                nc.vector.tensor_tensor(out=a[:, i, :], in0=k3[:], in1=y_of(c)[:, i, :], op=ADD)
+            arg[2, c] = a
+
+        def difference(c):
+            b, j0 = place(c)
+            t = sums.tile([P, CHUNK, H], F32, tag="total")
+            for i0 in range(0, CHUNK, PAIR):
+                nc.gpsimd.tensor_tensor(
+                    out=t[:, i0 : i0 + PAIR, :],
+                    in0=x_sb[:, b, j0 + i0 : j0 + i0 + PAIR, :],
+                    in1=x_sb[:, b, j0 + i0 + 1 : j0 + i0 + 1 + PAIR, :],
+                    op=SUB,
+                )
+            total[c] = t
+
+        def add_k1_k2(c):
+            b, j0 = place(c)
+            t = total[c]
+            for k_sb, weight in ((k1_sb, 1.0 / 6.0), (k2_sb, 1.0 / 3.0)):
+                nc.vector.scalar_tensor_tensor(
+                    out=t[:], in0=k_sb[:, b, j0 : j0 + CHUNK, :], scalar=weight, in1=t[:],
+                    op0=MULT, op1=ADD,
+                )
+
+        kk = {}
+
+        def two_k3_plus_k4(c):
+            for i in range(CHUNK):
+                acc = bank_kk.tile([P, H], F32)
+                product(acc, 1, c, i, True, False)
+                product(acc, 1, c, i, False, False)
+                product(acc, 2, c, i, False, True)
+                kk[c, i] = acc
+
+        def finish(c):
+            b, j0 = place(c)
+            t = total[c]
+            for i in range(CHUNK):
+                nc.vector.scalar_tensor_tensor(
+                    out=t[:, i, :], in0=kk[c, i][:], scalar=1.0 / 6.0, in1=t[:, i, :],
+                    op0=MULT, op1=ADD,
+                )
+            nc.sync.dma_start(out=by_partition(out[b])[:, j0 : j0 + CHUNK, :], in_=t[:])
+
+        def live(c):
+            return 0 <= c < N_CHUNKS
+
+        for i in range(-3, N_CHUNKS):
+            if live(i + 3):
+                halve_k2(i + 3)
+            if live(i + 2):
+                first_argument(i + 2)
+                turn(1, i + 2)
+                difference(i + 2)
+            if live(i):
+                quantise(2, i)
+            if live(i + 1):
+                quantise(1, i + 1)
+            if live(i):
+                two_k3_plus_k4(i)
+            if live(i + 1):
+                add_k1_k2(i + 1)
+                second_argument(i + 1)
+                turn(2, i + 1)
+            if live(i):
+                finish(i)

@@ -20,10 +20,8 @@ STEPS = 1024
 H = 512
 PACK = 4
 ROWS_PP = STEPS // P
-CHUNK = 4
-HALVES = ROWS_PP // CHUNK
-N_CHUNKS = SEQS * HALVES
-PAIR = 2
+CHUNK = 2
+N_CHUNKS = SEQS * ROWS_PP // CHUNK
 
 FLOPS = 2 * 2 * SEQS * STEPS * H * H
 
@@ -36,14 +34,17 @@ def tile_sindylossmixin_pa_t_kernel(
     def by_partition(rows):
         return rows.rearrange("(p j) f -> p j f", j=ROWS_PP)
 
+    def place(c):
+        first_tile = c * CHUNK
+        return first_tile // ROWS_PP, first_tile % ROWS_PP
+
     with ExitStack() as stack:
         stack.enter_context(tc.manual_schedule())
         keep = stack.enter_context(tc.tile_pool(name="keep", bufs=1))
         work = stack.enter_context(tc.tile_pool(name="work", bufs=2))
-        sums = stack.enter_context(tc.tile_pool(name="sums", bufs=4))
         bank_tr = stack.enter_context(tc.psum_pool(name="bank_tr", bufs=2))
-        bank_k3 = stack.enter_context(tc.psum_pool(name="bank_k3", bufs=2))
-        bank_kk = stack.enter_context(tc.psum_pool(name="bank_kk", bufs=4))
+        bank_k3 = stack.enter_context(tc.psum_pool(name="bank_k3", bufs=CHUNK))
+        bank_kk = stack.enter_context(tc.psum_pool(name="bank_kk", bufs=2 * CHUNK))
 
         x_sb = keep.tile([P, SEQS, ROWS_PP + 1, H], BF16)
         k1_sb = keep.tile([P, SEQS, ROWS_PP, H], BF16)
@@ -51,29 +52,33 @@ def tile_sindylossmixin_pa_t_kernel(
         w_words = keep.tile([P, 2 * H], U8, align_bytes=64)
         w_scales = keep.tile([P, H], U8, align_bytes=64)
         ident = keep.tile([P, P], F32)
+        warm = keep.tile([P, 1], F32)
 
-        def place(c):
-            return c // HALVES, CHUNK * (c % HALVES)
-
-        def load(dst, src, c):
+        def chunk_of(resident, c):
             b, j0 = place(c)
-            nc.sync.dma_start(out=dst[:, b, j0 : j0 + CHUNK, :], in_=src[:, j0 : j0 + CHUNK, :])
+            return resident[:, b, j0 : j0 + CHUNK, :]
 
         def load_x(c):
             b, j0 = place(c)
-            load(x_sb, by_partition(x[b, 0:STEPS, :]), c)
+            nc.sync.dma_start(
+                out=chunk_of(x_sb, c), in_=by_partition(x[b, 0:STEPS, :])[:, j0 : j0 + CHUNK, :]
+            )
             if j0 + CHUNK == ROWS_PP:
                 nc.sync.dma_start(
                     out=x_sb[:, b, ROWS_PP, :],
                     in_=by_partition(x[b, 1 : STEPS + 1, :])[:, ROWS_PP - 1, :],
                 )
 
-        def load_k(dst, src, c):
+        def load_k(resident, k, c):
             b, j0 = place(c)
-            load(dst, by_partition(src[b * STEPS : (b + 1) * STEPS, :]), c)
+            nc.sync.dma_start(
+                out=chunk_of(resident, c),
+                in_=by_partition(k[b * STEPS : (b + 1) * STEPS, :])[:, j0 : j0 + CHUNK, :],
+            )
 
         nc.vector.memset(w_scales[:].bitcast(I32), 0)
         make_identity(nc, ident[:])
+        nc.scalar.mul(warm[:], ident[:, 0:1], 0.5)
         load_x(0)
         load_k(k2_sb, k2, 0)
         nc.sync.dma_start(out=w_words[:].bitcast(I32), in_=coefficients_words[0].bitcast(I32))
@@ -89,39 +94,36 @@ def tile_sindylossmixin_pa_t_kernel(
             load_k(k1_sb, k1, c)
 
         half_k2 = {}
-        arg = {}
+        third_k2 = {}
+        argument = {}
         grouped = {}
         codes = {}
         scales = {}
+        step_back = {}
         total = {}
+        k3k3k4 = {}
 
-        def y_of(c):
-            b, j0 = place(c)
-            return x_sb[:, b, j0 : j0 + CHUNK, :]
-
-        def halve_k2(c):
-            b, j0 = place(c)
+        def scale_k2(c):
             h = work.tile([P, CHUNK, H], BF16, tag="half_k2")
-            nc.scalar.mul(h[:], k2_sb[:, b, j0 : j0 + CHUNK, :], 0.5)
+            nc.scalar.mul(h[:], chunk_of(k2_sb, c), 0.5)
             half_k2[c] = h
+            t = work.tile([P, CHUNK, H], F32, tag="third_k2")
+            nc.scalar.mul(t[:], chunk_of(k2_sb, c), 1.0 / 3.0)
+            third_k2[c] = t
 
         def first_argument(c):
-            a = work.tile([P, CHUNK, H], BF16, tag="arg1")
-            nc.vector.tensor_tensor(out=a[:], in0=y_of(c), in1=half_k2[c][:], op=ADD)
-            arg[1, c] = a
+            a = work.tile([P, CHUNK, H], BF16, tag="argument1")
+            nc.vector.tensor_tensor(out=a[:], in0=chunk_of(x_sb, c), in1=half_k2[c][:], op=ADD)
+            argument[1, c] = a
 
         def turn(stage, c):
+            turned = bank_tr.tile([P, CHUNK, 2, P], F32)
+            for i in range(CHUNK):
+                words = argument[stage, c][:, i, :].bitcast(F32)
+                for u in range(2):
+                    nc.tensor.transpose(turned[:, i, u, :], words[:, u : H // 2 : 2], ident[:])
             g = work.tile([P, CHUNK, P, PACK], BF16, tag="grouped%d" % stage, align_bytes=64)
-            for i0 in range(0, CHUNK, PAIR):
-                tr = bank_tr.tile([P, PAIR, 2, P], F32)
-                for i in range(PAIR):
-                    words = arg[stage, c][:, i0 + i, :].bitcast(F32)
-                    for u in range(2):
-                        nc.tensor.transpose(tr[:, i, u, :], words[:, u : H // 2 : 2], ident[:])
-                nc.scalar.copy(
-                    out=g[:, i0 : i0 + PAIR, :, :].bitcast(F32),
-                    in_=tr[:].rearrange("p i u r -> p i r u"),
-                )
+            nc.scalar.copy(out=g[:].bitcast(F32), in_=turned[:].rearrange("p i u r -> p i r u"))
             grouped[stage, c] = g
 
         def quantise(stage, c):
@@ -148,35 +150,31 @@ def tile_sindylossmixin_pa_t_kernel(
             )
 
         def second_argument(c):
-            a = work.tile([P, CHUNK, H], BF16, tag="arg2")
+            a = work.tile([P, CHUNK, H], BF16, tag="argument2")
             for i in range(CHUNK):
                 k3 = bank_k3.tile([P, H], F32)
                 product(k3, 1, c, i, True, True)
-                nc.vector.tensor_tensor(out=a[:, i, :], in0=k3[:], in1=y_of(c)[:, i, :], op=ADD)
-            arg[2, c] = a
-
-        def difference(c):
-            b, j0 = place(c)
-            t = sums.tile([P, CHUNK, H], F32, tag="total")
-            for i0 in range(0, CHUNK, PAIR):
-                nc.gpsimd.tensor_tensor(
-                    out=t[:, i0 : i0 + PAIR, :],
-                    in0=x_sb[:, b, j0 + i0 : j0 + i0 + PAIR, :],
-                    in1=x_sb[:, b, j0 + i0 + 1 : j0 + i0 + 1 + PAIR, :],
-                    op=SUB,
+                nc.vector.tensor_tensor(
+                    out=a[:, i, :], in0=k3[:], in1=chunk_of(x_sb, c)[:, i, :], op=ADD
                 )
+            argument[2, c] = a
+
+        def subtract_next_state(c):
+            b, j0 = place(c)
+            d = work.tile([P, CHUNK, H], F32, tag="step_back", bufs=1)
+            nc.gpsimd.tensor_tensor(
+                out=d[:], in0=chunk_of(x_sb, c), in1=x_sb[:, b, j0 + 1 : j0 + 1 + CHUNK, :], op=SUB
+            )
+            step_back[c] = d
+
+        def sum_of_inputs(c):
+            t = work.tile([P, CHUNK, H], F32, tag="total", bufs=4)
+            nc.vector.scalar_tensor_tensor(
+                out=t[:], in0=chunk_of(k1_sb, c), scalar=1.0 / 6.0, in1=third_k2[c][:],
+                op0=MULT, op1=ADD,
+            )
+            nc.vector.tensor_tensor(out=t[:], in0=t[:], in1=step_back[c][:], op=ADD)
             total[c] = t
-
-        def add_k1_k2(c):
-            b, j0 = place(c)
-            t = total[c]
-            for k_sb, weight in ((k1_sb, 1.0 / 6.0), (k2_sb, 1.0 / 3.0)):
-                nc.vector.scalar_tensor_tensor(
-                    out=t[:], in0=k_sb[:, b, j0 : j0 + CHUNK, :], scalar=weight, in1=t[:],
-                    op0=MULT, op1=ADD,
-                )
-
-        kk = {}
 
         def two_k3_plus_k4(c):
             for i in range(CHUNK):
@@ -184,14 +182,14 @@ def tile_sindylossmixin_pa_t_kernel(
                 product(acc, 1, c, i, True, False)
                 product(acc, 1, c, i, False, False)
                 product(acc, 2, c, i, False, True)
-                kk[c, i] = acc
+                k3k3k4[c, i] = acc
 
         def finish(c):
             b, j0 = place(c)
             t = total[c]
             for i in range(CHUNK):
                 nc.vector.scalar_tensor_tensor(
-                    out=t[:, i, :], in0=kk[c, i][:], scalar=1.0 / 6.0, in1=t[:, i, :],
+                    out=t[:, i, :], in0=k3k3k4[c, i][:], scalar=1.0 / 6.0, in1=t[:, i, :],
                     op0=MULT, op1=ADD,
                 )
             nc.sync.dma_start(out=by_partition(out[b])[:, j0 : j0 + CHUNK, :], in_=t[:])
@@ -199,22 +197,23 @@ def tile_sindylossmixin_pa_t_kernel(
         def live(c):
             return 0 <= c < N_CHUNKS
 
-        for i in range(-3, N_CHUNKS):
-            if live(i + 3):
-                halve_k2(i + 3)
-            if live(i + 2):
-                first_argument(i + 2)
-                turn(1, i + 2)
-                difference(i + 2)
-            if live(i):
-                quantise(2, i)
-            if live(i + 1):
-                quantise(1, i + 1)
-            if live(i):
-                two_k3_plus_k4(i)
-            if live(i + 1):
-                add_k1_k2(i + 1)
-                second_argument(i + 1)
-                turn(2, i + 1)
-            if live(i):
-                finish(i)
+        for c in range(-3, N_CHUNKS):
+            if live(c + 2):
+                first_argument(c + 2)
+                turn(1, c + 2)
+                subtract_next_state(c + 2)
+            if live(c + 3):
+                scale_k2(c + 3)
+            if live(c + 1):
+                quantise(1, c + 1)
+            if live(c):
+                quantise(2, c)
+            if live(c + 1):
+                sum_of_inputs(c + 1)
+                second_argument(c + 1)
+            if live(c):
+                two_k3_plus_k4(c)
+            if live(c + 1):
+                turn(2, c + 1)
+            if live(c):
+                finish(c)

@@ -39,7 +39,6 @@ def tile_sindylossmixin_pa_t_kernel(
         return first_tile // ROWS_PP, first_tile % ROWS_PP
 
     with ExitStack() as stack:
-        stack.enter_context(tc.manual_schedule())
         keep = stack.enter_context(tc.tile_pool(name="keep", bufs=1))
         work = stack.enter_context(tc.tile_pool(name="work", bufs=2))
         bank_tr = stack.enter_context(tc.psum_pool(name="bank_tr", bufs=2))

@@ -39,6 +39,7 @@ def tile_sindylossmixin_pa_t_kernel(
         return first_tile // ROWS_PP, first_tile % ROWS_PP
 
     with ExitStack() as stack:
+        stack.enter_context(tc.manual_schedule())
         keep = stack.enter_context(tc.tile_pool(name="keep", bufs=1))
         work = stack.enter_context(tc.tile_pool(name="work", bufs=2))
         bank_tr = stack.enter_context(tc.psum_pool(name="bank_tr", bufs=2))
@@ -100,12 +101,15 @@ def tile_sindylossmixin_pa_t_kernel(
         scales = {}
         step_back = {}
         total = {}
+        k3 = {}
         k3k3k4 = {}
 
-        def scale_k2(c):
+        def halve_k2(c):
             h = work.tile([P, CHUNK, H], BF16, tag="half_k2")
             nc.scalar.mul(h[:], chunk_of(k2_sb, c), 0.5)
             half_k2[c] = h
+
+        def third_of_k2(c):
             t = work.tile([P, CHUNK, H], F32, tag="third_k2")
             nc.scalar.mul(t[:], chunk_of(k2_sb, c), 1.0 / 3.0)
             third_k2[c] = t
@@ -126,8 +130,8 @@ def tile_sindylossmixin_pa_t_kernel(
             grouped[stage, c] = g
 
         def quantise(stage, c):
-            q = work.tile([P, CHUNK * P], U32, tag="codes%d" % stage, bufs=3, align_bytes=64)
-            s = work.tile([P, CHUNK * P], U8, tag="scales%d" % stage, bufs=3, align_bytes=64)
+            q = work.tile([P, CHUNK * P], U32, tag="codes%d" % stage, bufs=4, align_bytes=64)
+            s = work.tile([P, CHUNK * P], U8, tag="scales%d" % stage, bufs=4, align_bytes=64)
             nc.vector.quantize_mx(
                 out=q[:].bitcast(FP8X4),
                 scales=s[:],
@@ -148,13 +152,17 @@ def tile_sindylossmixin_pa_t_kernel(
                 stop=stop,
             )
 
+        def first_product(c):
+            for i in range(CHUNK):
+                acc = bank_k3.tile([P, H], F32)
+                product(acc, 1, c, i, True, True)
+                k3[c, i] = acc
+
         def second_argument(c):
             a = work.tile([P, CHUNK, H], BF16, tag="argument2")
             for i in range(CHUNK):
-                k3 = bank_k3.tile([P, H], F32)
-                product(k3, 1, c, i, True, True)
                 nc.vector.tensor_tensor(
-                    out=a[:, i, :], in0=k3[:], in1=chunk_of(x_sb, c)[:, i, :], op=ADD
+                    out=a[:, i, :], in0=k3[c, i][:], in1=chunk_of(x_sb, c)[:, i, :], op=ADD
                 )
             argument[2, c] = a
 
@@ -167,7 +175,7 @@ def tile_sindylossmixin_pa_t_kernel(
             step_back[c] = d
 
         def sum_of_inputs(c):
-            t = work.tile([P, CHUNK, H], F32, tag="total", bufs=4)
+            t = work.tile([P, CHUNK, H], F32, tag="total", bufs=5)
             nc.vector.scalar_tensor_tensor(
                 out=t[:], in0=chunk_of(k1_sb, c), scalar=1.0 / 6.0, in1=third_k2[c][:],
                 op0=MULT, op1=ADD,
@@ -191,28 +199,32 @@ def tile_sindylossmixin_pa_t_kernel(
                     out=t[:, i, :], in0=k3k3k4[c, i][:], scalar=1.0 / 6.0, in1=t[:, i, :],
                     op0=MULT, op1=ADD,
                 )
-            nc.sync.dma_start(out=by_partition(out[b])[:, j0 : j0 + CHUNK, :], in_=t[:])
+                nc.sync.dma_start(out=by_partition(out[b])[:, j0 + i, :], in_=t[:, i, :])
 
         def live(c):
             return 0 <= c < N_CHUNKS
 
-        for c in range(-3, N_CHUNKS):
-            if live(c + 2):
-                first_argument(c + 2)
-                turn(1, c + 2)
-                subtract_next_state(c + 2)
+        for c in range(-5, N_CHUNKS):
+            if live(c + 5):
+                halve_k2(c + 5)
             if live(c + 3):
-                scale_k2(c + 3)
-            if live(c + 1):
-                quantise(1, c + 1)
-            if live(c):
-                quantise(2, c)
-            if live(c + 1):
-                sum_of_inputs(c + 1)
-                second_argument(c + 1)
-            if live(c):
-                two_k3_plus_k4(c)
-            if live(c + 1):
-                turn(2, c + 1)
+                third_of_k2(c + 3)
             if live(c):
                 finish(c)
+            if live(c + 2):
+                second_argument(c + 2)
+                turn(2, c + 2)
+            if live(c + 4):
+                first_argument(c + 4)
+                turn(1, c + 4)
+            if live(c + 2):
+                sum_of_inputs(c + 2)
+            if live(c + 3):
+                subtract_next_state(c + 3)
+                quantise(1, c + 3)
+            if live(c + 2):
+                quantise(2, c + 2)
+            if live(c + 3):
+                first_product(c + 3)
+            if live(c + 2):
+                two_k3_plus_k4(c + 2)

@@ -94,7 +94,6 @@ def tile_sindylossmixin_pa_t_kernel(
             load_k(k1_sb, k1, c)
 
         half_k2 = {}
-        third_k2 = {}
         argument = {}
         grouped = {}
         codes = {}
@@ -108,11 +107,6 @@ def tile_sindylossmixin_pa_t_kernel(
             h = work.tile([P, CHUNK, H], BF16, tag="half_k2")
             nc.scalar.mul(h[:], chunk_of(k2_sb, c), 0.5)
             half_k2[c] = h
-
-        def third_of_k2(c):
-            t = work.tile([P, CHUNK, H], F32, tag="third_k2")
-            nc.scalar.mul(t[:], chunk_of(k2_sb, c), 1.0 / 3.0)
-            third_k2[c] = t
 
         def first_argument(c):
             a = work.tile([P, CHUNK, H], BF16, tag="argument1")
@@ -174,14 +168,19 @@ def tile_sindylossmixin_pa_t_kernel(
             )
             step_back[c] = d
 
-        def sum_of_inputs(c):
+        def sum_of_stages(c):
             t = work.tile([P, CHUNK, H], F32, tag="total", bufs=5)
             nc.vector.scalar_tensor_tensor(
-                out=t[:], in0=chunk_of(k1_sb, c), scalar=1.0 / 6.0, in1=third_k2[c][:],
+                out=t[:], in0=chunk_of(k1_sb, c), scalar=0.5, in1=chunk_of(k2_sb, c),
                 op0=MULT, op1=ADD,
             )
-            nc.vector.tensor_tensor(out=t[:], in0=t[:], in1=step_back[c][:], op=ADD)
             total[c] = t
+
+        def sum_of_inputs(c):
+            t = total[c]
+            nc.vector.scalar_tensor_tensor(
+                out=t[:], in0=t[:], scalar=1.0 / 3.0, in1=step_back[c][:], op0=MULT, op1=ADD,
+            )
 
         def two_k3_plus_k4(c):
             for i in range(CHUNK):
@@ -204,27 +203,27 @@ def tile_sindylossmixin_pa_t_kernel(
         def live(c):
             return 0 <= c < N_CHUNKS
 
-        for c in range(-5, N_CHUNKS):
-            if live(c + 5):
-                halve_k2(c + 5)
-            if live(c + 3):
-                third_of_k2(c + 3)
+        for c in range(-6, N_CHUNKS):
+            if live(c + 6):
+                halve_k2(c + 6)
             if live(c):
                 finish(c)
+            if live(c + 3):
+                second_argument(c + 3)
+                turn(2, c + 3)
             if live(c + 2):
-                second_argument(c + 2)
-                turn(2, c + 2)
+                sum_of_stages(c + 2)
+            if live(c + 5):
+                first_argument(c + 5)
+                turn(1, c + 5)
             if live(c + 4):
-                first_argument(c + 4)
-                turn(1, c + 4)
+                quantise(1, c + 4)
             if live(c + 2):
+                quantise(2, c + 2)
                 sum_of_inputs(c + 2)
             if live(c + 3):
                 subtract_next_state(c + 3)
-                quantise(1, c + 3)
-            if live(c + 2):
-                quantise(2, c + 2)
-            if live(c + 3):
-                first_product(c + 3)
+            if live(c + 4):
+                first_product(c + 4)
             if live(c + 2):
                 two_k3_plus_k4(c + 2)

@@ -93,7 +93,7 @@ def tile_sindylossmixin_pa_t_kernel(
             load_k(k2_sb, k2, c)
             load_k(k1_sb, k1, c)
 
-        half_k2 = {}
+        two_y = {}
         argument = {}
         grouped = {}
         codes = {}
@@ -103,14 +103,14 @@ def tile_sindylossmixin_pa_t_kernel(
         k3 = {}
         k3k3k4 = {}
 
-        def halve_k2(c):
-            h = work.tile([P, CHUNK, H], BF16, tag="half_k2")
-            nc.scalar.mul(h[:], chunk_of(k2_sb, c), 0.5)
-            half_k2[c] = h
+        def double_y(c):
+            h = work.tile([P, CHUNK, H], BF16, tag="two_y")
+            nc.scalar.mul(h[:], chunk_of(x_sb, c), 2.0)
+            two_y[c] = h
 
         def first_argument(c):
             a = work.tile([P, CHUNK, H], BF16, tag="argument1")
-            nc.vector.tensor_tensor(out=a[:], in0=chunk_of(x_sb, c), in1=half_k2[c][:], op=ADD)
+            nc.vector.tensor_tensor(out=a[:], in0=two_y[c][:], in1=chunk_of(k2_sb, c), op=ADD)
             argument[1, c] = a
 
         def turn(stage, c):
@@ -155,8 +155,9 @@ def tile_sindylossmixin_pa_t_kernel(
         def second_argument(c):
             a = work.tile([P, CHUNK, H], BF16, tag="argument2")
             for i in range(CHUNK):
-                nc.vector.tensor_tensor(
-                    out=a[:, i, :], in0=k3[c, i][:], in1=chunk_of(x_sb, c)[:, i, :], op=ADD
+                nc.vector.scalar_tensor_tensor(
+                    out=a[:, i, :], in0=k3[c, i][:], scalar=0.5, in1=chunk_of(x_sb, c)[:, i, :],
+                    op0=MULT, op1=ADD,
                 )
             argument[2, c] = a
 
@@ -186,7 +187,6 @@ def tile_sindylossmixin_pa_t_kernel(
             for i in range(CHUNK):
                 acc = bank_kk.tile([P, H], F32)
                 product(acc, 1, c, i, True, False)
-                product(acc, 1, c, i, False, False)
                 product(acc, 2, c, i, False, True)
                 k3k3k4[c, i] = acc
 
@@ -205,7 +205,7 @@ def tile_sindylossmixin_pa_t_kernel(
 
         for c in range(-6, N_CHUNKS):
             if live(c + 6):
-                halve_k2(c + 6)
+                double_y(c + 6)
             if live(c):
                 finish(c)
             if live(c + 3):

@@ -52,6 +52,8 @@ def tile_sindylossmixin_pa_t_kernel(
         w_words = keep.tile([P, 2 * H], U8, align_bytes=64)
         w_scales = keep.tile([P, H], U8, align_bytes=64)
         ident = keep.tile([P, P], F32)
+        ident_bf = keep.tile([P, P], BF16)
+        weights = keep.tile([P, 3, P], BF16)
         warm = keep.tile([P, 1], F32)
 
         def chunk_of(resident, c):
@@ -79,6 +81,9 @@ def tile_sindylossmixin_pa_t_kernel(
         nc.vector.memset(w_scales[:].bitcast(I32), 0)
         make_identity(nc, ident[:])
         nc.scalar.mul(warm[:], ident[:, 0:1], 0.5)
+        make_identity(nc, ident_bf[:])
+        for slot, factor in enumerate((6.0, -6.0, 2.0)):
+            nc.scalar.mul(weights[:, slot, :], ident_bf[:], factor)
         load_x(0)
         load_k(k2_sb, k2, 0)
         nc.sync.dma_start(out=w_words[:].bitcast(I32), in_=coefficients_words[0].bitcast(I32))
@@ -114,7 +119,7 @@ def tile_sindylossmixin_pa_t_kernel(
             argument[1, c] = a
 
         def turn(stage, c):
-            turned = bank_tr.tile([P, CHUNK, 2, P], F32)
+            turned = bank_tr.tile([P, CHUNK, 2, P], F32, tag="turned")
             for i in range(CHUNK):
                 words = argument[stage, c][:, i, :].bitcast(F32)
                 for u in range(2):
@@ -183,6 +188,24 @@ def tile_sindylossmixin_pa_t_kernel(
                 out=t[:], in0=t[:], scalar=1.0 / 3.0, in1=step_back[c][:], op0=MULT, op1=ADD,
             )
 
+        def sum_on_tensor_engine(c):
+            b, j0 = place(c)
+            t = work.tile([P, CHUNK, H], F32, tag="total", bufs=5)
+            for i in range(CHUNK):
+                acc = bank_tr.tile([P, H], F32, tag="turned")
+                terms = (
+                    (weights[:, 0, :], x_sb[:, b, j0 + i, :]),
+                    (weights[:, 1, :], x_sb[:, b, j0 + i + 1, :]),
+                    (ident_bf[:], k1_sb[:, b, j0 + i, :]),
+                    (weights[:, 2, :], k2_sb[:, b, j0 + i, :]),
+                )
+                for n, (factor, term) in enumerate(terms):
+                    nc.tensor.matmul(
+                        out=acc[:], lhsT=factor, rhs=term, start=n == 0, stop=n == len(terms) - 1
+                    )
+                nc.scalar.mul(t[:, i, :], acc[:], 1.0 / 6.0)
+            total[c] = t
+
         def two_k3_plus_k4(c):
             for i in range(CHUNK):
                 acc = bank_kk.tile([P, H], F32)
@@ -203,15 +226,20 @@ def tile_sindylossmixin_pa_t_kernel(
         def live(c):
             return 0 <= c < N_CHUNKS
 
+        def on_tensor_engine(c):
+            return c % 5 == 3
+
         for c in range(-6, N_CHUNKS):
             if live(c + 6):
                 double_y(c + 6)
+            if live(c + 2) and on_tensor_engine(c + 2):
+                sum_on_tensor_engine(c + 2)
             if live(c):
                 finish(c)
             if live(c + 3):
                 second_argument(c + 3)
                 turn(2, c + 3)
-            if live(c + 2):
+            if live(c + 2) and not on_tensor_engine(c + 2):
                 sum_of_stages(c + 2)
             if live(c + 5):
                 first_argument(c + 5)
@@ -220,8 +248,9 @@ def tile_sindylossmixin_pa_t_kernel(
                 quantise(1, c + 4)
             if live(c + 2):
                 quantise(2, c + 2)
+            if live(c + 2) and not on_tensor_engine(c + 2):
                 sum_of_inputs(c + 2)
-            if live(c + 3):
+            if live(c + 3) and not on_tensor_engine(c + 3):
                 subtract_next_state(c + 3)
             if live(c + 4):
                 first_product(c + 4)

@@ -56,6 +56,9 @@ def tile_sindylossmixin_pa_t_kernel(
         weights = keep.tile([P, 3, P], BF16)
         warm = keep.tile([P, 1], F32)
 
+        def by_vector(c):
+            return CHUNK - 1 if c % 3 == 0 else CHUNK
+
         def chunk_of(resident, c):
             b, j0 = place(c)
             return resident[:, b, j0 : j0 + CHUNK, :]
@@ -168,30 +171,35 @@ def tile_sindylossmixin_pa_t_kernel(
 
         def subtract_next_state(c):
             b, j0 = place(c)
+            n = by_vector(c)
             d = work.tile([P, CHUNK, H], F32, tag="step_back", bufs=1)
             nc.gpsimd.tensor_tensor(
-                out=d[:], in0=chunk_of(x_sb, c), in1=x_sb[:, b, j0 + 1 : j0 + 1 + CHUNK, :], op=SUB
+                out=d[:, 0:n, :], in0=x_sb[:, b, j0 : j0 + n, :],
+                in1=x_sb[:, b, j0 + 1 : j0 + 1 + n, :], op=SUB,
             )
             step_back[c] = d
 
         def sum_of_stages(c):
+            n = by_vector(c)
             t = work.tile([P, CHUNK, H], F32, tag="total", bufs=5)
             nc.vector.scalar_tensor_tensor(
-                out=t[:], in0=chunk_of(k1_sb, c), scalar=0.5, in1=chunk_of(k2_sb, c),
-                op0=MULT, op1=ADD,
+                out=t[:, 0:n, :], in0=chunk_of(k1_sb, c)[:, 0:n, :], scalar=0.5,
+                in1=chunk_of(k2_sb, c)[:, 0:n, :], op0=MULT, op1=ADD,
             )
             total[c] = t
 
         def sum_of_inputs(c):
+            n = by_vector(c)
             t = total[c]
             nc.vector.scalar_tensor_tensor(
-                out=t[:], in0=t[:], scalar=1.0 / 3.0, in1=step_back[c][:], op0=MULT, op1=ADD,
+                out=t[:, 0:n, :], in0=t[:, 0:n, :], scalar=1.0 / 3.0, in1=step_back[c][:, 0:n, :],
+                op0=MULT, op1=ADD,
             )
 
         def sum_on_tensor_engine(c):
             b, j0 = place(c)
-            t = work.tile([P, CHUNK, H], F32, tag="total", bufs=5)
-            for i in range(CHUNK):
+            t = total[c]
+            for i in range(by_vector(c), CHUNK):
                 acc = bank_tr.tile([P, H], F32, tag="turned")
                 terms = (
                     (weights[:, 0, :], x_sb[:, b, j0 + i, :]),
@@ -204,7 +212,6 @@ def tile_sindylossmixin_pa_t_kernel(
                         out=acc[:], lhsT=factor, rhs=term, start=n == 0, stop=n == len(terms) - 1
                     )
                 nc.scalar.mul(t[:, i, :], acc[:], 1.0 / 6.0)
-            total[c] = t
 
         def two_k3_plus_k4(c):
             for i in range(CHUNK):
@@ -226,21 +233,18 @@ def tile_sindylossmixin_pa_t_kernel(
         def live(c):
             return 0 <= c < N_CHUNKS
 
-        def on_tensor_engine(c):
-            return c % 5 == 3
 
         for c in range(-6, N_CHUNKS):
             if live(c + 6):
                 double_y(c + 6)
-            if live(c + 2) and on_tensor_engine(c + 2):
-                sum_on_tensor_engine(c + 2)
             if live(c):
                 finish(c)
             if live(c + 3):
                 second_argument(c + 3)
                 turn(2, c + 3)
-            if live(c + 2) and not on_tensor_engine(c + 2):
+            if live(c + 2):
                 sum_of_stages(c + 2)
+                sum_on_tensor_engine(c + 2)
             if live(c + 5):
                 first_argument(c + 5)
                 turn(1, c + 5)
@@ -248,9 +252,8 @@ def tile_sindylossmixin_pa_t_kernel(
                 quantise(1, c + 4)
             if live(c + 2):
                 quantise(2, c + 2)
-            if live(c + 2) and not on_tensor_engine(c + 2):
                 sum_of_inputs(c + 2)
-            if live(c + 3) and not on_tensor_engine(c + 3):
+            if live(c + 3):
                 subtract_next_state(c + 3)
             if live(c + 4):
                 first_product(c + 4)

@@ -42,9 +42,9 @@ def tile_sindylossmixin_pa_t_kernel(
         stack.enter_context(tc.manual_schedule())
         keep = stack.enter_context(tc.tile_pool(name="keep", bufs=1))
         work = stack.enter_context(tc.tile_pool(name="work", bufs=2))
-        bank_tr = stack.enter_context(tc.psum_pool(name="bank_tr", bufs=2))
+        bank_tr = stack.enter_context(tc.psum_pool(name="bank_tr", bufs=4))
         bank_k3 = stack.enter_context(tc.psum_pool(name="bank_k3", bufs=CHUNK))
-        bank_kk = stack.enter_context(tc.psum_pool(name="bank_kk", bufs=2 * CHUNK))
+        bank_kk = stack.enter_context(tc.psum_pool(name="bank_kk", bufs=CHUNK))
 
         x_sb = keep.tile([P, SEQS, ROWS_PP + 1, H], BF16)
         k1_sb = keep.tile([P, SEQS, ROWS_PP, H], BF16)
@@ -102,6 +102,7 @@ def tile_sindylossmixin_pa_t_kernel(
             load_k(k1_sb, k1, c)
 
         two_y = {}
+        wide_k2 = {}
         argument = {}
         grouped = {}
         codes = {}
@@ -111,15 +112,32 @@ def tile_sindylossmixin_pa_t_kernel(
         k3 = {}
         k3k3k4 = {}
 
+        def by_word_slot(rows):
+            return rows.rearrange("p i (q t) -> p i t q", t=PACK)
+
         def double_y(c):
-            h = work.tile([P, CHUNK, H], BF16, tag="two_y")
-            nc.scalar.mul(h[:], chunk_of(x_sb, c), 2.0)
+            h = work.tile([P, CHUNK, PACK, P], F32, tag="two_y")
+            nc.scalar.mul(h[:], by_word_slot(chunk_of(x_sb, c)), 2.0)
             two_y[c] = h
+            w = work.tile([P, CHUNK, PACK, P], F32, tag="wide_k2")
+            nc.scalar.copy(out=w[:], in_=by_word_slot(chunk_of(k2_sb, c)))
+            wide_k2[c] = w
 
         def first_argument(c):
-            a = work.tile([P, CHUNK, H], BF16, tag="argument1")
-            nc.vector.tensor_tensor(out=a[:], in0=two_y[c][:], in1=chunk_of(k2_sb, c), op=ADD)
-            argument[1, c] = a
+            g = work.tile([P, CHUNK, P, PACK], BF16, tag="grouped1", align_bytes=64)
+            for i in range(CHUNK):
+                summed = bank_tr.tile([P, PACK, P], F32, tag="turned")
+                for t in range(PACK):
+                    nc.tensor.matmul(
+                        out=summed[:, t, :], lhsT=two_y[c][:, i, t, :], rhs=ident[:],
+                        is_transpose=True, start=True, stop=False,
+                    )
+                    nc.tensor.matmul(
+                        out=summed[:, t, :], lhsT=wide_k2[c][:, i, t, :], rhs=ident[:],
+                        is_transpose=True, start=False, stop=True,
+                    )
+                nc.scalar.copy(out=g[:, i, :, :], in_=summed[:].rearrange("p t r -> p r t"))
+            grouped[1, c] = g
 
         def turn(stage, c):
             turned = bank_tr.tile([P, CHUNK, 2, P], F32, tag="turned")
@@ -172,7 +190,7 @@ def tile_sindylossmixin_pa_t_kernel(
         def subtract_next_state(c):
             b, j0 = place(c)
             n = by_vector(c)
-            d = work.tile([P, CHUNK, H], F32, tag="step_back", bufs=1)
+            d = work.tile([P, CHUNK, H], F32, tag="step_back", bufs=2)
             nc.gpsimd.tensor_tensor(
                 out=d[:, 0:n, :], in0=x_sb[:, b, j0 : j0 + n, :],
                 in1=x_sb[:, b, j0 + 1 : j0 + 1 + n, :], op=SUB,
@@ -234,28 +252,27 @@ def tile_sindylossmixin_pa_t_kernel(
             return 0 <= c < N_CHUNKS
 
 
-        for c in range(-6, N_CHUNKS):
-            if live(c + 6):
-                double_y(c + 6)
+        for c in range(-5, N_CHUNKS):
+            if live(c + 5):
+                double_y(c + 5)
+            if live(c + 4):
+                first_argument(c + 4)
+            if live(c + 2):
+                second_argument(c + 2)
+                turn(2, c + 2)
             if live(c):
                 finish(c)
             if live(c + 3):
-                second_argument(c + 3)
-                turn(2, c + 3)
-            if live(c + 2):
-                sum_of_stages(c + 2)
-                sum_on_tensor_engine(c + 2)
-            if live(c + 5):
-                first_argument(c + 5)
-                turn(1, c + 5)
-            if live(c + 4):
-                quantise(1, c + 4)
-            if live(c + 2):
-                quantise(2, c + 2)
-                sum_of_inputs(c + 2)
+                sum_of_stages(c + 3)
+                sum_on_tensor_engine(c + 3)
+                quantise(1, c + 3)
+            if live(c + 1):
+                quantise(2, c + 1)
             if live(c + 3):
-                subtract_next_state(c + 3)
+                sum_of_inputs(c + 3)
             if live(c + 4):
-                first_product(c + 4)
-            if live(c + 2):
-                two_k3_plus_k4(c + 2)
+                subtract_next_state(c + 4)
+            if live(c + 3):
+                first_product(c + 3)
+            if live(c + 1):
+                two_k3_plus_k4(c + 1)

@@ -63,22 +63,20 @@ def tile_sindylossmixin_pa_t_kernel(
             b, j0 = place(c)
             return resident[:, b, j0 : j0 + CHUNK, :]
 
-        def load_x(c):
-            b, j0 = place(c)
+        def load_x(b, j0, n):
             nc.sync.dma_start(
-                out=chunk_of(x_sb, c), in_=by_partition(x[b, 0:STEPS, :])[:, j0 : j0 + CHUNK, :]
+                out=x_sb[:, b, j0 : j0 + n, :], in_=by_partition(x[b, 0:STEPS, :])[:, j0 : j0 + n, :]
             )
-            if j0 + CHUNK == ROWS_PP:
+            if j0 + n == ROWS_PP:
                 nc.sync.dma_start(
                     out=x_sb[:, b, ROWS_PP, :],
                     in_=by_partition(x[b, 1 : STEPS + 1, :])[:, ROWS_PP - 1, :],
                 )
 
-        def load_k(resident, k, c):
-            b, j0 = place(c)
+        def load_k(resident, k, b, j0, n):
             nc.sync.dma_start(
-                out=chunk_of(resident, c),
-                in_=by_partition(k[b * STEPS : (b + 1) * STEPS, :])[:, j0 : j0 + CHUNK, :],
+                out=resident[:, b, j0 : j0 + n, :],
+                in_=by_partition(k[b * STEPS : (b + 1) * STEPS, :])[:, j0 : j0 + n, :],
             )
 
         nc.vector.memset(w_scales[:].bitcast(I32), 0)
@@ -87,35 +85,38 @@ def tile_sindylossmixin_pa_t_kernel(
         make_identity(nc, ident_bf[:])
         for slot, factor in enumerate((6.0, -6.0, 2.0)):
             nc.scalar.mul(weights[:, slot, :], ident_bf[:], factor)
-        load_x(0)
-        load_k(k2_sb, k2, 0)
+        load_x(0, 0, CHUNK)
+        load_k(k2_sb, k2, 0, 0, CHUNK)
+        load_k(k1_sb, k1, 0, 0, CHUNK)
         nc.sync.dma_start(out=w_words[:].bitcast(I32), in_=coefficients_words[0].bitcast(I32))
         for quad in range(4):
             nc.sync.dma_start(
                 out=w_scales[32 * quad : 32 * quad + 4, :].bitcast(I32),
                 in_=coefficients_scales[0, 4 * quad : 4 * quad + 4, :].bitcast(I32),
             )
-        load_k(k1_sb, k1, 0)
-        for c in range(1, N_CHUNKS):
-            load_x(c)
-            load_k(k2_sb, k2, c)
-            load_k(k1_sb, k1, c)
+        for j0 in range(CHUNK, ROWS_PP, CHUNK):
+            load_x(0, j0, CHUNK)
+            load_k(k2_sb, k2, 0, j0, CHUNK)
+            load_k(k1_sb, k1, 0, j0, CHUNK)
+        for b in range(1, SEQS):
+            load_x(b, 0, ROWS_PP)
+            load_k(k2_sb, k2, b, 0, ROWS_PP)
+            load_k(k1_sb, k1, b, 0, ROWS_PP)
 
         two_y = {}
         wide_k2 = {}
-        argument = {}
+        argument2 = {}
         grouped = {}
         codes = {}
-        scales = {}
         step_back = {}
         total = {}
-        k3 = {}
+        two_k3 = {}
         k3k3k4 = {}
 
         def by_word_slot(rows):
             return rows.rearrange("p i (q t) -> p i t q", t=PACK)
 
-        def double_y(c):
+        def widen(c):
             h = work.tile([P, CHUNK, PACK, P], F32, tag="two_y")
             nc.scalar.mul(h[:], by_word_slot(chunk_of(x_sb, c)), 2.0)
             two_y[c] = h
@@ -123,8 +124,11 @@ def tile_sindylossmixin_pa_t_kernel(
             nc.scalar.copy(out=w[:], in_=by_word_slot(chunk_of(k2_sb, c)))
             wide_k2[c] = w
 
-        def first_argument(c):
-            g = work.tile([P, CHUNK, P, PACK], BF16, tag="grouped1", align_bytes=64)
+        def new_grouped(c):
+            g = work.tile([P, 2, CHUNK, P, PACK], BF16, tag="grouped", align_bytes=64)
+            grouped[c] = g
+
+        def first_argument(c, g):
             for i in range(CHUNK):
                 summed = bank_tr.tile([P, PACK, P], F32, tag="turned")
                 for t in range(PACK):
@@ -136,36 +140,47 @@ def tile_sindylossmixin_pa_t_kernel(
                         out=summed[:, t, :], lhsT=wide_k2[c][:, i, t, :], rhs=ident[:],
                         is_transpose=True, start=False, stop=True,
                     )
-                nc.scalar.copy(out=g[:, i, :, :], in_=summed[:].rearrange("p t r -> p r t"))
-            grouped[1, c] = g
+                nc.scalar.copy(out=g[:, 0, i, :, :], in_=summed[:].rearrange("p t r -> p r t"))
 
-        def turn(stage, c):
+        def second_argument(c):
+            a = work.tile([P, CHUNK, H], BF16, tag="argument2")
+            for i in range(CHUNK):
+                nc.vector.scalar_tensor_tensor(
+                    out=a[:, i, :], in0=two_k3[c, i][:], scalar=0.5, in1=chunk_of(x_sb, c)[:, i, :],
+                    op0=MULT, op1=ADD,
+                )
+            argument2[c] = a
+
+        def turn_second_argument(c, g):
             turned = bank_tr.tile([P, CHUNK, 2, P], F32, tag="turned")
             for i in range(CHUNK):
-                words = argument[stage, c][:, i, :].bitcast(F32)
+                words = argument2[c][:, i, :].bitcast(F32)
                 for u in range(2):
                     nc.tensor.transpose(turned[:, i, u, :], words[:, u : H // 2 : 2], ident[:])
-            g = work.tile([P, CHUNK, P, PACK], BF16, tag="grouped%d" % stage, align_bytes=64)
-            nc.scalar.copy(out=g[:].bitcast(F32), in_=turned[:].rearrange("p i u r -> p i r u"))
-            grouped[stage, c] = g
-
-        def quantise(stage, c):
-            q = work.tile([P, CHUNK * P], U32, tag="codes%d" % stage, bufs=4, align_bytes=64)
-            s = work.tile([P, CHUNK * P], U8, tag="scales%d" % stage, bufs=4, align_bytes=64)
-            nc.vector.quantize_mx(
-                out=q[:].bitcast(FP8X4),
-                scales=s[:],
-                in_=grouped[stage, c][:].rearrange("p i r t -> p (i r t)"),
+            nc.scalar.copy(
+                out=g[:, 1, :, :, :].bitcast(F32), in_=turned[:].rearrange("p i u r -> p i r u")
             )
-            codes[stage, c] = q
-            scales[stage, c] = s
+
+        def quantise(g, chunk_by_stage):
+            q = work.tile([P, 2 * CHUNK * P], U32, tag="codes", bufs=4, align_bytes=64)
+            s = work.tile([P, 2 * CHUNK * P], U8, tag="scales", bufs=4, align_bytes=64)
+            lo = (min(chunk_by_stage) - 1) * CHUNK * P
+            hi = max(chunk_by_stage) * CHUNK * P
+            nc.vector.quantize_mx(
+                out=q[:, lo:hi].bitcast(FP8X4),
+                scales=s[:, lo:hi],
+                in_=g[:].rearrange("p s i r t -> p (s i r t)")[:, PACK * lo : PACK * hi],
+            )
+            for stage, c in chunk_by_stage.items():
+                codes[stage, c] = (q, s, (stage - 1) * CHUNK * P)
 
         def product(acc, stage, c, i, start, stop):
-            rows = slice(i * P, (i + 1) * P)
+            q, s, first = codes[stage, c]
+            rows = slice(first + i * P, first + (i + 1) * P)
             nc.tensor.matmul_mx(
                 out=acc[:],
-                lhsT=codes[stage, c][:, rows].bitcast(FP8X4),
-                lhsT_scale=scales[stage, c][:, rows],
+                lhsT=q[:, rows].bitcast(FP8X4),
+                lhsT_scale=s[:, rows],
                 rhs=w_words[:].bitcast(FP4X4),
                 rhs_scale=w_scales[:],
                 start=start,
@@ -176,16 +191,7 @@ def tile_sindylossmixin_pa_t_kernel(
             for i in range(CHUNK):
                 acc = bank_k3.tile([P, H], F32)
                 product(acc, 1, c, i, True, True)
-                k3[c, i] = acc
-
-        def second_argument(c):
-            a = work.tile([P, CHUNK, H], BF16, tag="argument2")
-            for i in range(CHUNK):
-                nc.vector.scalar_tensor_tensor(
-                    out=a[:, i, :], in0=k3[c, i][:], scalar=0.5, in1=chunk_of(x_sb, c)[:, i, :],
-                    op0=MULT, op1=ADD,
-                )
-            argument[2, c] = a
+                two_k3[c, i] = acc
 
         def subtract_next_state(c):
             b, j0 = place(c)
@@ -199,7 +205,7 @@ def tile_sindylossmixin_pa_t_kernel(
 
         def sum_of_stages(c):
             n = by_vector(c)
-            t = work.tile([P, CHUNK, H], F32, tag="total", bufs=5)
+            t = work.tile([P, CHUNK, H], F32, tag="total", bufs=8)
             nc.vector.scalar_tensor_tensor(
                 out=t[:, 0:n, :], in0=chunk_of(k1_sb, c)[:, 0:n, :], scalar=0.5,
                 in1=chunk_of(k2_sb, c)[:, 0:n, :], op0=MULT, op1=ADD,
@@ -251,27 +257,35 @@ def tile_sindylossmixin_pa_t_kernel(
         def live(c):
             return 0 <= c < N_CHUNKS
 
+        def round_of_sums(k):
+            return k - 5
 
-        for c in range(-5, N_CHUNKS):
+        subtract_next_state(0)
+        sum_of_stages(0)
+        sum_on_tensor_engine(0)
+        for c in range(-6, N_CHUNKS):
+            sums = [k for k in range(N_CHUNKS) if round_of_sums(k) == c]
             if live(c + 5):
-                double_y(c + 5)
+                widen(c + 5)
+            if live(c + 4) or live(c + 2):
+                new_grouped(c)
             if live(c + 4):
-                first_argument(c + 4)
+                first_argument(c + 4, grouped[c])
             if live(c + 2):
                 second_argument(c + 2)
-                turn(2, c + 2)
+                turn_second_argument(c + 2, grouped[c])
             if live(c):
                 finish(c)
-            if live(c + 3):
-                sum_of_stages(c + 3)
-                sum_on_tensor_engine(c + 3)
-                quantise(1, c + 3)
-            if live(c + 1):
-                quantise(2, c + 1)
-            if live(c + 3):
-                sum_of_inputs(c + 3)
-            if live(c + 4):
-                subtract_next_state(c + 4)
+            ready = {stage: k for stage, k in ((1, c + 3), (2, c + 1)) if live(k)}
+            if ready:
+                quantise(grouped[c - 1], ready)
+            for k in sums:
+                if live(k + 1):
+                    sum_of_stages(k + 1)
+                    sum_on_tensor_engine(k + 1)
+                sum_of_inputs(k)
+                if live(k + 1):
+                    subtract_next_state(k + 1)
             if live(c + 3):
                 first_product(c + 3)
             if live(c + 1):

@@ -22,6 +22,8 @@ PACK = 4
 ROWS_PP = STEPS // P
 CHUNK = 2
 N_CHUNKS = SEQS * ROWS_PP // CHUNK
+BY_TENSOR = 192
+BY_VECTOR = CHUNK * H - BY_TENSOR
 
 FLOPS = 2 * 2 * SEQS * STEPS * H * H
 
@@ -56,8 +58,8 @@ def tile_sindylossmixin_pa_t_kernel(
         weights = keep.tile([P, 3, P], BF16)
         warm = keep.tile([P, 1], F32)
 
-        def by_vector(c):
-            return CHUNK - 1 if c % 3 == 0 else CHUNK
+        def flat(rows):
+            return rows.rearrange("p i f -> p (i f)")
 
         def chunk_of(resident, c):
             b, j0 = place(c)
@@ -195,47 +197,43 @@ def tile_sindylossmixin_pa_t_kernel(
 
         def subtract_next_state(c):
             b, j0 = place(c)
-            n = by_vector(c)
-            d = work.tile([P, CHUNK, H], F32, tag="step_back", bufs=2)
+            d = work.tile([P, BY_VECTOR], F32, tag="step_back", bufs=2)
             nc.gpsimd.tensor_tensor(
-                out=d[:, 0:n, :], in0=x_sb[:, b, j0 : j0 + n, :],
-                in1=x_sb[:, b, j0 + 1 : j0 + 1 + n, :], op=SUB,
+                out=d[:], in0=flat(x_sb[:, b, j0 : j0 + CHUNK, :])[:, 0:BY_VECTOR],
+                in1=flat(x_sb[:, b, j0 + 1 : j0 + 1 + CHUNK, :])[:, 0:BY_VECTOR], op=SUB,
             )
             step_back[c] = d
 
         def sum_of_stages(c):
-            n = by_vector(c)
             t = work.tile([P, CHUNK, H], F32, tag="total", bufs=8)
             nc.vector.scalar_tensor_tensor(
-                out=t[:, 0:n, :], in0=chunk_of(k1_sb, c)[:, 0:n, :], scalar=0.5,
-                in1=chunk_of(k2_sb, c)[:, 0:n, :], op0=MULT, op1=ADD,
+                out=flat(t[:])[:, 0:BY_VECTOR], in0=flat(chunk_of(k1_sb, c))[:, 0:BY_VECTOR],
+                scalar=0.5, in1=flat(chunk_of(k2_sb, c))[:, 0:BY_VECTOR], op0=MULT, op1=ADD,
             )
             total[c] = t
 
         def sum_of_inputs(c):
-            n = by_vector(c)
-            t = total[c]
+            t = flat(total[c][:])[:, 0:BY_VECTOR]
             nc.vector.scalar_tensor_tensor(
-                out=t[:, 0:n, :], in0=t[:, 0:n, :], scalar=1.0 / 3.0, in1=step_back[c][:, 0:n, :],
-                op0=MULT, op1=ADD,
+                out=t, in0=t, scalar=1.0 / 3.0, in1=step_back[c][:], op0=MULT, op1=ADD
             )
 
         def sum_on_tensor_engine(c):
             b, j0 = place(c)
-            t = total[c]
-            for i in range(by_vector(c), CHUNK):
-                acc = bank_tr.tile([P, H], F32, tag="turned")
-                terms = (
-                    (weights[:, 0, :], x_sb[:, b, j0 + i, :]),
-                    (weights[:, 1, :], x_sb[:, b, j0 + i + 1, :]),
-                    (ident_bf[:], k1_sb[:, b, j0 + i, :]),
-                    (weights[:, 2, :], k2_sb[:, b, j0 + i, :]),
+            j = j0 + CHUNK - 1
+            cols = slice(H - BY_TENSOR, H)
+            acc = bank_tr.tile([P, BY_TENSOR], F32, tag="turned")
+            terms = (
+                (weights[:, 0, :], x_sb[:, b, j, cols]),
+                (weights[:, 1, :], x_sb[:, b, j + 1, cols]),
+                (ident_bf[:], k1_sb[:, b, j, cols]),
+                (weights[:, 2, :], k2_sb[:, b, j, cols]),
+            )
+            for n, (factor, term) in enumerate(terms):
+                nc.tensor.matmul(
+                    out=acc[:], lhsT=factor, rhs=term, start=n == 0, stop=n == len(terms) - 1
                 )
-                for n, (factor, term) in enumerate(terms):
-                    nc.tensor.matmul(
-                        out=acc[:], lhsT=factor, rhs=term, start=n == 0, stop=n == len(terms) - 1
-                    )
-                nc.scalar.mul(t[:, i, :], acc[:], 1.0 / 6.0)
+            nc.scalar.mul(total[c][:, CHUNK - 1, cols], acc[:], 1.0 / 6.0)
 
         def two_k3_plus_k4(c):
             for i in range(CHUNK):

@@ -205,7 +205,7 @@ def tile_sindylossmixin_pa_t_kernel(
             step_back[c] = d
 
         def sum_of_stages(c):
-            t = work.tile([P, CHUNK, H], F32, tag="total", bufs=8)
+            t = work.tile([P, CHUNK, H], F32, tag="total", bufs=9)
             nc.vector.scalar_tensor_tensor(
                 out=flat(t[:])[:, 0:BY_VECTOR], in0=flat(chunk_of(k1_sb, c))[:, 0:BY_VECTOR],
                 scalar=0.5, in1=flat(chunk_of(k2_sb, c))[:, 0:BY_VECTOR], op0=MULT, op1=ADD,
@@ -255,14 +255,9 @@ def tile_sindylossmixin_pa_t_kernel(
         def live(c):
             return 0 <= c < N_CHUNKS
 
-        def round_of_sums(k):
-            return k - 5
-
         subtract_next_state(0)
-        sum_of_stages(0)
-        sum_on_tensor_engine(0)
+        subtract_next_state(1)
         for c in range(-6, N_CHUNKS):
-            sums = [k for k in range(N_CHUNKS) if round_of_sums(k) == c]
             if live(c + 5):
                 widen(c + 5)
             if live(c + 4) or live(c + 2):
@@ -277,13 +272,13 @@ def tile_sindylossmixin_pa_t_kernel(
             ready = {stage: k for stage, k in ((1, c + 3), (2, c + 1)) if live(k)}
             if ready:
                 quantise(grouped[c - 1], ready)
-            for k in sums:
-                if live(k + 1):
-                    sum_of_stages(k + 1)
-                    sum_on_tensor_engine(k + 1)
-                sum_of_inputs(k)
-                if live(k + 1):
-                    subtract_next_state(k + 1)
+            if live(c + 6):
+                sum_of_stages(c + 6)
+                sum_on_tensor_engine(c + 6)
+            if live(c + 2):
+                sum_of_inputs(c + 2)
+            if live(c + 2 + 2):
+                subtract_next_state(c + 2 + 2)
             if live(c + 3):
                 first_product(c + 3)
             if live(c + 1):

@@ -90,16 +90,19 @@ def tile_sindylossmixin_pa_t_kernel(
         load_x(0, 0, CHUNK)
         load_k(k2_sb, k2, 0, 0, CHUNK)
         load_k(k1_sb, k1, 0, 0, CHUNK)
-        nc.sync.dma_start(out=w_words[:].bitcast(I32), in_=coefficients_words[0].bitcast(I32))
-        for quad in range(4):
-            nc.sync.dma_start(
-                out=w_scales[32 * quad : 32 * quad + 4, :].bitcast(I32),
-                in_=coefficients_scales[0, 4 * quad : 4 * quad + 4, :].bitcast(I32),
-            )
         for j0 in range(CHUNK, ROWS_PP, CHUNK):
             load_x(0, j0, CHUNK)
             load_k(k2_sb, k2, 0, j0, CHUNK)
             load_k(k1_sb, k1, 0, j0, CHUNK)
+            if j0 == CHUNK:
+                nc.sync.dma_start(
+                    out=w_words[:].bitcast(I32), in_=coefficients_words[0].bitcast(I32)
+                )
+                for quad in range(4):
+                    nc.sync.dma_start(
+                        out=w_scales[32 * quad : 32 * quad + 4, :].bitcast(I32),
+                        in_=coefficients_scales[0, 4 * quad : 4 * quad + 4, :].bitcast(I32),
+                    )
         for b in range(1, SEQS):
             load_x(b, 0, ROWS_PP)
             load_k(k2_sb, k2, b, 0, ROWS_PP)
@@ -146,7 +149,7 @@ def tile_sindylossmixin_pa_t_kernel(
 
         def second_argument(c):
             a = work.tile([P, CHUNK, H], BF16, tag="argument2")
-            for i in range(CHUNK):
+            for i in reversed(range(CHUNK)):
                 nc.vector.scalar_tensor_tensor(
                     out=a[:, i, :], in0=two_k3[c, i][:], scalar=0.5, in1=chunk_of(x_sb, c)[:, i, :],
                     op0=MULT, op1=ADD,
@@ -155,7 +158,7 @@ def tile_sindylossmixin_pa_t_kernel(
 
         def turn_second_argument(c, g):
             turned = bank_tr.tile([P, CHUNK, 2, P], F32, tag="turned")
-            for i in range(CHUNK):
+            for i in reversed(range(CHUNK)):
                 words = argument2[c][:, i, :].bitcast(F32)
                 for u in range(2):
                     nc.tensor.transpose(turned[:, i, u, :], words[:, u : H // 2 : 2], ident[:])
@@ -272,13 +275,13 @@ def tile_sindylossmixin_pa_t_kernel(
             ready = {stage: k for stage, k in ((1, c + 3), (2, c + 1)) if live(k)}
             if ready:
                 quantise(grouped[c - 1], ready)
-            if live(c + 6):
-                sum_of_stages(c + 6)
-                sum_on_tensor_engine(c + 6)
             if live(c + 2):
                 sum_of_inputs(c + 2)
             if live(c + 2 + 2):
                 subtract_next_state(c + 2 + 2)
+            if live(c + 6):
+                sum_of_stages(c + 6)
+                sum_on_tensor_engine(c + 6)
             if live(c + 3):
                 first_product(c + 3)
             if live(c + 1):

@@ -270,15 +270,18 @@ def tile_sindylossmixin_pa_t_kernel(
             if live(c + 2):
                 second_argument(c + 2)
                 turn_second_argument(c + 2, grouped[c])
+            ready = {stage: k for stage, k in ((1, c + 3), (2, c + 1)) if live(k)}
+            quantise_first = not live(c + 4 + 2)
+            if ready and quantise_first:
+                quantise(grouped[c - 1], ready)
             if live(c):
                 finish(c)
-            ready = {stage: k for stage, k in ((1, c + 3), (2, c + 1)) if live(k)}
-            if ready:
+            if ready and not quantise_first:
                 quantise(grouped[c - 1], ready)
-            if live(c + 2):
-                sum_of_inputs(c + 2)
-            if live(c + 2 + 2):
-                subtract_next_state(c + 2 + 2)
+            if live(c + 4):
+                sum_of_inputs(c + 4)
+            if live(c + 4 + 2):
+                subtract_next_state(c + 4 + 2)
             if live(c + 6):
                 sum_of_stages(c + 6)
                 sum_on_tensor_engine(c + 6)

@@ -258,8 +258,6 @@ def tile_sindylossmixin_pa_t_kernel(
         def live(c):
             return 0 <= c < N_CHUNKS
 
-        subtract_next_state(0)
-        subtract_next_state(1)
         for c in range(-6, N_CHUNKS):
             if live(c + 5):
                 widen(c + 5)

@@ -103,7 +103,11 @@ def tile_sindylossmixin_pa_t_kernel(
                         out=w_scales[32 * quad : 32 * quad + 4, :].bitcast(I32),
                         in_=coefficients_scales[0, 4 * quad : 4 * quad + 4, :].bitcast(I32),
                     )
-        for b in range(1, SEQS):
+        for j0 in range(0, ROWS_PP, CHUNK):
+            load_x(1, j0, CHUNK)
+            load_k(k2_sb, k2, 1, j0, CHUNK)
+            load_k(k1_sb, k1, 1, j0, CHUNK)
+        for b in range(2, SEQS):
             load_x(b, 0, ROWS_PP)
             load_k(k2_sb, k2, b, 0, ROWS_PP)
             load_k(k1_sb, k1, b, 0, ROWS_PP)

from contextlib import ExitStack

import concourse.mybir as mybir
from concourse.masks import make_identity

F32 = mybir.dt.float32
BF16 = mybir.dt.bfloat16
I32 = mybir.dt.int32
U32 = mybir.dt.uint32
U8 = mybir.dt.uint8
FP8X4 = mybir.dt.float8_e4m3fn_x4
FP4X4 = mybir.dt.float4_e2m1fn_x4
ADD = mybir.AluOpType.add
SUB = mybir.AluOpType.subtract
MULT = mybir.AluOpType.mult

P = 128
SEQS = 4
STEPS = 1024
H = 512
PACK = 4
ROWS_PP = STEPS // P
CHUNK = 2
N_CHUNKS = SEQS * ROWS_PP // CHUNK
BY_TENSOR = 192
BY_VECTOR = CHUNK * H - BY_TENSOR

FLOPS = 2 * 2 * SEQS * STEPS * H * H


def tile_sindylossmixin_pa_t_kernel(
    tc, x, k1, k2, coefficients_words, coefficients_scales, out
):
    nc = tc.nc

    def by_partition(rows):
        return rows.rearrange("(p j) f -> p j f", j=ROWS_PP)

    def place(c):
        first_tile = c * CHUNK
        return first_tile // ROWS_PP, first_tile % ROWS_PP

    with ExitStack() as stack:
        stack.enter_context(tc.manual_schedule())
        keep = stack.enter_context(tc.tile_pool(name="keep", bufs=1))
        work = stack.enter_context(tc.tile_pool(name="work", bufs=2))
        bank_tr = stack.enter_context(tc.psum_pool(name="bank_tr", bufs=4))
        bank_k3 = stack.enter_context(tc.psum_pool(name="bank_k3", bufs=CHUNK))
        bank_kk = stack.enter_context(tc.psum_pool(name="bank_kk", bufs=CHUNK))

        x_sb = keep.tile([P, SEQS, ROWS_PP + 1, H], BF16)
        k1_sb = keep.tile([P, SEQS, ROWS_PP, H], BF16)
        k2_sb = keep.tile([P, SEQS, ROWS_PP, H], BF16)
        w_words = keep.tile([P, 2 * H], U8, align_bytes=64)
        w_scales = keep.tile([P, H], U8, align_bytes=64)
        ident = keep.tile([P, P], F32)
        ident_bf = keep.tile([P, P], BF16)
        weights = keep.tile([P, 3, P], BF16)
        warm = keep.tile([P, 1], F32)

        def flat(rows):
            return rows.rearrange("p i f -> p (i f)")

        def chunk_of(resident, c):
            b, j0 = place(c)
            return resident[:, b, j0 : j0 + CHUNK, :]

        def load_x(b, j0, n):
            nc.sync.dma_start(
                out=x_sb[:, b, j0 : j0 + n, :], in_=by_partition(x[b, 0:STEPS, :])[:, j0 : j0 + n, :]
            )
            if j0 + n == ROWS_PP:
                nc.sync.dma_start(
                    out=x_sb[:, b, ROWS_PP, :],
                    in_=by_partition(x[b, 1 : STEPS + 1, :])[:, ROWS_PP - 1, :],
                )

        def load_k(resident, k, b, j0, n):
            nc.sync.dma_start(
                out=resident[:, b, j0 : j0 + n, :],
                in_=by_partition(k[b * STEPS : (b + 1) * STEPS, :])[:, j0 : j0 + n, :],
            )

        nc.vector.memset(w_scales[:].bitcast(I32), 0)
        make_identity(nc, ident[:])
        nc.scalar.mul(warm[:], ident[:, 0:1], 0.5)
        make_identity(nc, ident_bf[:])
        for slot, factor in enumerate((6.0, -6.0, 2.0)):
            nc.scalar.mul(weights[:, slot, :], ident_bf[:], factor)
        load_x(0, 0, CHUNK)
        load_k(k2_sb, k2, 0, 0, CHUNK)
        load_k(k1_sb, k1, 0, 0, CHUNK)
        for j0 in range(CHUNK, ROWS_PP, CHUNK):
            load_x(0, j0, CHUNK)
            load_k(k2_sb, k2, 0, j0, CHUNK)
            load_k(k1_sb, k1, 0, j0, CHUNK)
            if j0 == CHUNK:
                nc.sync.dma_start(
                    out=w_words[:].bitcast(I32), in_=coefficients_words[0].bitcast(I32)
                )
                for quad in range(4):
                    nc.sync.dma_start(
                        out=w_scales[32 * quad : 32 * quad + 4, :].bitcast(I32),
                        in_=coefficients_scales[0, 4 * quad : 4 * quad + 4, :].bitcast(I32),
                    )
        for j0 in range(0, ROWS_PP, CHUNK):
            load_x(1, j0, CHUNK)
            load_k(k2_sb, k2, 1, j0, CHUNK)
            load_k(k1_sb, k1, 1, j0, CHUNK)
        for b in range(2, SEQS):
            load_x(b, 0, ROWS_PP)
            load_k(k2_sb, k2, b, 0, ROWS_PP)
            load_k(k1_sb, k1, b, 0, ROWS_PP)

        two_y = {}
        wide_k2 = {}
        argument2 = {}
        grouped = {}
        codes = {}
        step_back = {}
        total = {}
        two_k3 = {}
        k3k3k4 = {}

        def by_word_slot(rows):
            return rows.rearrange("p i (q t) -> p i t q", t=PACK)

        def widen(c):
            h = work.tile([P, CHUNK, PACK, P], F32, tag="two_y")
            nc.scalar.mul(h[:], by_word_slot(chunk_of(x_sb, c)), 2.0)
            two_y[c] = h
            w = work.tile([P, CHUNK, PACK, P], F32, tag="wide_k2")
            nc.scalar.copy(out=w[:], in_=by_word_slot(chunk_of(k2_sb, c)))
            wide_k2[c] = w

        def new_grouped(c):
            g = work.tile([P, 2, CHUNK, P, PACK], BF16, tag="grouped", align_bytes=64)
            grouped[c] = g

        def first_argument(c, g):
            for i in range(CHUNK):
                summed = bank_tr.tile([P, PACK, P], F32, tag="turned")
                for t in range(PACK):
                    nc.tensor.matmul(
                        out=summed[:, t, :], lhsT=two_y[c][:, i, t, :], rhs=ident[:],
                        is_transpose=True, start=True, stop=False,
                    )
                    nc.tensor.matmul(
                        out=summed[:, t, :], lhsT=wide_k2[c][:, i, t, :], rhs=ident[:],
                        is_transpose=True, start=False, stop=True,
                    )
                nc.scalar.copy(out=g[:, 0, i, :, :], in_=summed[:].rearrange("p t r -> p r t"))

        def second_argument(c):
            a = work.tile([P, CHUNK, H], BF16, tag="argument2")
            for i in reversed(range(CHUNK)):
                nc.vector.scalar_tensor_tensor(
                    out=a[:, i, :], in0=two_k3[c, i][:], scalar=0.5, in1=chunk_of(x_sb, c)[:, i, :],
                    op0=MULT, op1=ADD,
                )
            argument2[c] = a

        def turn_second_argument(c, g):
            turned = bank_tr.tile([P, CHUNK, 2, P], F32, tag="turned")
            for i in reversed(range(CHUNK)):
                words = argument2[c][:, i, :].bitcast(F32)
                for u in range(2):
                    nc.tensor.transpose(turned[:, i, u, :], words[:, u : H // 2 : 2], ident[:])
            nc.scalar.copy(
                out=g[:, 1, :, :, :].bitcast(F32), in_=turned[:].rearrange("p i u r -> p i r u")
            )

        def quantise(g, chunk_by_stage):
            q = work.tile([P, 2 * CHUNK * P], U32, tag="codes", bufs=4, align_bytes=64)
            s = work.tile([P, 2 * CHUNK * P], U8, tag="scales", bufs=4, align_bytes=64)
            lo = (min(chunk_by_stage) - 1) * CHUNK * P
            hi = max(chunk_by_stage) * CHUNK * P
            nc.vector.quantize_mx(
                out=q[:, lo:hi].bitcast(FP8X4),
                scales=s[:, lo:hi],
                in_=g[:].rearrange("p s i r t -> p (s i r t)")[:, PACK * lo : PACK * hi],
            )
            for stage, c in chunk_by_stage.items():
                codes[stage, c] = (q, s, (stage - 1) * CHUNK * P)

        def product(acc, stage, c, i, start, stop):
            q, s, first = codes[stage, c]
            rows = slice(first + i * P, first + (i + 1) * P)
            nc.tensor.matmul_mx(
                out=acc[:],
                lhsT=q[:, rows].bitcast(FP8X4),
                lhsT_scale=s[:, rows],
                rhs=w_words[:].bitcast(FP4X4),
                rhs_scale=w_scales[:],
                start=start,
                stop=stop,
            )

        def first_product(c):
            for i in range(CHUNK):
                acc = bank_k3.tile([P, H], F32)
                product(acc, 1, c, i, True, True)
                two_k3[c, i] = acc

        def subtract_next_state(c):
            b, j0 = place(c)
            d = work.tile([P, BY_VECTOR], F32, tag="step_back", bufs=2)
            nc.gpsimd.tensor_tensor(
                out=d[:], in0=flat(x_sb[:, b, j0 : j0 + CHUNK, :])[:, 0:BY_VECTOR],
                in1=flat(x_sb[:, b, j0 + 1 : j0 + 1 + CHUNK, :])[:, 0:BY_VECTOR], op=SUB,
            )
            step_back[c] = d

        def sum_of_stages(c):
            t = work.tile([P, CHUNK, H], F32, tag="total", bufs=9)
            nc.vector.scalar_tensor_tensor(
                out=flat(t[:])[:, 0:BY_VECTOR], in0=flat(chunk_of(k1_sb, c))[:, 0:BY_VECTOR],
                scalar=0.5, in1=flat(chunk_of(k2_sb, c))[:, 0:BY_VECTOR], op0=MULT, op1=ADD,
            )
            total[c] = t

        def sum_of_inputs(c):
            t = flat(total[c][:])[:, 0:BY_VECTOR]
            nc.vector.scalar_tensor_tensor(
                out=t, in0=t, scalar=1.0 / 3.0, in1=step_back[c][:], op0=MULT, op1=ADD
            )

        def sum_on_tensor_engine(c):
            b, j0 = place(c)
            j = j0 + CHUNK - 1
            cols = slice(H - BY_TENSOR, H)
            acc = bank_tr.tile([P, BY_TENSOR], F32, tag="turned")
            terms = (
                (weights[:, 0, :], x_sb[:, b, j, cols]),
                (weights[:, 1, :], x_sb[:, b, j + 1, cols]),
                (ident_bf[:], k1_sb[:, b, j, cols]),
                (weights[:, 2, :], k2_sb[:, b, j, cols]),
            )
            for n, (factor, term) in enumerate(terms):
                nc.tensor.matmul(
                    out=acc[:], lhsT=factor, rhs=term, start=n == 0, stop=n == len(terms) - 1
                )
            nc.scalar.mul(total[c][:, CHUNK - 1, cols], acc[:], 1.0 / 6.0)

        def two_k3_plus_k4(c):
            for i in range(CHUNK):
                acc = bank_kk.tile([P, H], F32)
                product(acc, 1, c, i, True, False)
                product(acc, 2, c, i, False, True)
                k3k3k4[c, i] = acc

        def finish(c):
            b, j0 = place(c)
            t = total[c]
            for i in range(CHUNK):
                nc.vector.scalar_tensor_tensor(
                    out=t[:, i, :], in0=k3k3k4[c, i][:], scalar=1.0 / 6.0, in1=t[:, i, :],
                    op0=MULT, op1=ADD,
                )
                nc.sync.dma_start(out=by_partition(out[b])[:, j0 + i, :], in_=t[:, i, :])

        def live(c):
            return 0 <= c < N_CHUNKS

        for c in range(-6, N_CHUNKS):
            if live(c + 5):
                widen(c + 5)
            if live(c + 4) or live(c + 2):
                new_grouped(c)
            if live(c + 4):
                first_argument(c + 4, grouped[c])
            if live(c + 2):
                second_argument(c + 2)
                turn_second_argument(c + 2, grouped[c])
            ready = {stage: k for stage, k in ((1, c + 3), (2, c + 1)) if live(k)}
            quantise_first = not live(c + 4 + 2)
            if ready and quantise_first:
                quantise(grouped[c - 1], ready)
            if live(c):
                finish(c)
            if ready and not quantise_first:
                quantise(grouped[c - 1], ready)
            if live(c + 4):
                sum_of_inputs(c + 4)
            if live(c + 4 + 2):
                subtract_next_state(c + 4 + 2)
            if live(c + 6):
                sum_of_stages(c + 6)
                sum_on_tensor_engine(c + 6)
            if live(c + 3):
                first_product(c + 3)
            if live(c + 1):
                two_k3_plus_k4(c + 1)
